import numpy as np
import ml_dtypes


def mxq(x, axis, fmt="e4m3"):
    dtype, down = {"e4m3": (ml_dtypes.float8_e4m3fn, 7), "e5m2": (ml_dtypes.float8_e5m2, 14)}[fmt]
    v = np.moveaxis(np.asarray(x, np.float32).astype(ml_dtypes.bfloat16).astype(np.float64), axis, -1)
    blocks = v.reshape(v.shape[:-1] + (-1, 32))
    amax = np.abs(blocks).max(-1, keepdims=True)
    byte = np.maximum(np.where(amax > 0, np.frexp(amax)[1] - 1 + 127, 0) - down, 1)
    scale = np.exp2(byte - 127.0)
    codes = (blocks / scale).astype(np.float32).astype(dtype).astype(np.float64)
    return np.moveaxis((codes * scale).reshape(v.shape), -1, axis)


WIDE = False


def mx_kscale(k):
    if not WIDE:
        return np.ones(k)
    levels = np.array([10, -10, 5, -5, 0])
    if k % 512:
        return np.exp2(np.random.permutation(np.resize(levels, k // 32))).repeat(32)
    a = np.empty((k // 512, 16))
    for p in range(k // 512):
        a[p, :8] = np.random.permutation(np.resize(levels, 8))
        for g in range(8):
            far = levels[np.abs(levels - a[p, g]) >= 10]
            a[p, g + 8] = far[np.random.randint(len(far))]
    return np.exp2(a.ravel()).repeat(32)


BF16 = ml_dtypes.bfloat16


def bf(x):
    return np.asarray(x, np.float32).astype(BF16)


def f64(x):
    return np.asarray(x).astype(np.float64)


B, C, HH, WW, NH = 4, 512, 16, 16, 8
N = HH * WW
DH = C // NH
HALF = C // 2


def pos_encoding():
    positions = np.arange(N, dtype=np.float64)
    depths = np.arange(HALF, dtype=np.float64) / HALF
    angle_rates = 1.0 / (10000.0 ** depths)
    angle_rads = positions[:, None] * angle_rates[None, :]
    return np.concatenate([np.sin(angle_rads), np.cos(angle_rads)], axis=-1)


def heads(t):
    return t.reshape(B, N, NH, DH).transpose(0, 2, 1, 3)


def setup_inputs():
    bound = np.sqrt(6.0 / (C + 3 * C))
    s = mx_kscale(C)
    u = s / s.min()
    return {"x": bf(np.random.standard_normal((B, C, HH, WW)) * u[None, :, None, None]),
            "W_qkv": bf(np.random.uniform(-bound, bound, (3 * C, C)) / u[None, :])}


def reference(x, W_qkv):
    xt = f64(x).reshape(B, C, N) + pos_encoding().T[None]
    tokens = xt.transpose(0, 2, 1)
    qkv = mxq(tokens, 2, "e4m3") @ mxq(f64(W_qkv), 1, "e4m3").T
    q, k, v = np.split(qkv, 3, axis=-1)
    return heads(q), heads(k), heads(v)

@@ -1,0 +1,239 @@
+import math
+from contextlib import ExitStack
+
+import concourse.mybir as mybir
+
+F32 = mybir.dt.float32
+BF16 = mybir.dt.bfloat16
+I32 = mybir.dt.int32
+U32 = mybir.dt.uint32
+U8 = mybir.dt.uint8
+FP8X4 = mybir.dt.float8_e4m3fn_x4
+ALU = mybir.AluOpType
+ACT = mybir.ActivationFunctionType
+
+P = 128
+HALF_P = P // 2
+PACK = 4
+IMAGES = 4
+CHANNELS = 512
+POSITIONS = 256
+HEAD_DIM = 64
+BANK = 512
+
+PAIR = 2
+PAIRS = IMAGES // PAIR
+RUN = 4
+ROWS = POSITIONS // RUN
+TABLE_CHUNKS = 4
+
+UNIT_HEADS = 4
+UNIT_COLS = UNIT_HEADS * HEAD_DIM
+UNIT_BLOCKS = UNIT_COLS // P
+UNITS = 6
+UNITS_PER_OUTPUT = 2
+COPY_AHEAD = 4
+QUANTISE_AHEAD = 2
+
+RATES = CHANNELS // 2
+ROUND = 1.5 * 2.0**23
+
+FLOPS = 2 * IMAGES * POSITIONS * CHANNELS * UNITS * UNIT_COLS
+
+
+def tile_multiheadselfattention_pa_kernel(tc, x, W_qkv, out_0, out_1, out_2):
+    nc = tc.nc
+    outs = (out_0, out_1, out_2)
+    with ExitStack() as pools:
+        keep = pools.enter_context(tc.tile_pool(name="keep", bufs=1))
+        stage_pool = pools.enter_context(tc.tile_pool(name="stage", bufs=6))
+        psum = pools.enter_context(tc.psum_pool(name="psum", bufs=8))
+        pools.enter_context(tc.manual_schedule())
+
+        x_rows = keep.tile([P, IMAGES * PACK, POSITIONS], BF16)
+        w_rows = keep.tile([P, UNITS, UNIT_BLOCKS, CHANNELS], BF16)
+
+        def load_x(pair):
+            nc.sync.dma_start(
+                out=x_rows[:, pair * PAIR * PACK : (pair + 1) * PAIR * PACK, :].rearrange(
+                    "q (b t) n -> q b (t n)", b=PAIR
+                ),
+                in_=x[pair * PAIR : (pair + 1) * PAIR].rearrange(
+                    "b (q t) h w -> q b (t h w)", t=PACK
+                ),
+            )
+
+        load_x(0)
+        for unit in range(UNITS):
+            nc.sync.dma_start(
+                out=w_rows[:, unit],
+                in_=W_qkv[unit * UNIT_COLS : (unit + 1) * UNIT_COLS, :].rearrange(
+                    "(g o) c -> o g c", o=P
+                ),
+            )
+        load_x(1)
+
+        chan_int = keep.tile([P, PACK], I32)
+        for first in (0, HALF_P):
+            nc.gpsimd.iota(
+                chan_int[first : first + HALF_P], pattern=[[1, PACK]], base=0, channel_multiplier=PACK
+            )
+        base = keep.tile([P, PACK], F32)
+        nc.gpsimd.memset(base[:], 10000.0)
+        exponent = keep.tile([P, PACK], F32)
+        nc.vector.tensor_scalar_mul(out=exponent[:], in0=chan_int[:], scalar1=-1.0 / RATES)
+        rate = keep.tile([P, PACK], F32)
+        nc.gpsimd.tensor_tensor(out=rate[:], in0=base[:], in1=exponent[:], op=ALU.pow)
+        own_index = keep.tile([P, 1], I32)
+        nc.gpsimd.iota(own_index[:], pattern=[[1, 1]], base=0, channel_multiplier=1)
+        phase = keep.tile([P, 1], F32)
+        nc.vector.memset(phase[0:HALF_P], 0.0)
+        nc.vector.memset(phase[HALF_P:P], 0.25)
+
+        warm = keep.tile([P, 2], F32)
+        nc.vector.memset(warm[:, 0:1], 0.0)
+        nc.scalar.activation(out=warm[:, 1:2], in_=warm[:, 0:1], func=ACT.Sin)
+
+        ones = keep.tile([P, POSITIONS], F32)
+        nc.vector.memset(ones[:], 1.0)
+        count = keep.tile([P, POSITIONS], F32)
+        nc.vector.tensor_tensor_scan(
+            out=count[:], data0=ones[:], data1=ones[:], initial=-1.0, op0=ALU.mult, op1=ALU.add
+        )
+
+        turn_rate = keep.tile([P, PACK], F32)
+        nc.vector.tensor_scalar_mul(out=turn_rate[:], in0=rate[:], scalar1=1.0 / (2.0 * math.pi))
+        turns = keep.tile([P, PACK, POSITIONS], F32)
+        for t in range(PACK):
+            nc.vector.tensor_scalar(
+                out=turns[:, t, :],
+                in0=count[:],
+                scalar1=turn_rate[:, t : t + 1],
+                scalar2=phase[:],
+                op0=ALU.mult,
+                op1=ALU.add,
+            )
+        whole = keep.tile([P, PACK, POSITIONS], F32)
+        nc.vector.tensor_scalar(
+            out=whole[:], in0=turns[:], scalar1=ROUND, scalar2=ROUND, op0=ALU.add, op1=ALU.subtract
+        )
+        frac = keep.tile([P, PACK, POSITIONS], F32)
+        nc.vector.tensor_tensor(out=frac[:], in0=turns[:], in1=whole[:], op=ALU.subtract)
+        index = keep.tile([P, 1], F32)
+        nc.vector.tensor_copy(out=index[:], in_=own_index[:])
+        ident = keep.tile([P, P], F32)
+        nc.vector.tensor_scalar(
+            out=ident[:], in0=count[:, 0:P], scalar1=index[:], scalar2=None, op0=ALU.is_equal
+        )
+        pe = keep.tile([P, PAIR * PACK, POSITIONS], F32)
+        pe_parts = pe[:].rearrange("q (b t) n -> q b t n", b=PAIR)
+        chunk_positions = POSITIONS // TABLE_CHUNKS
+        for chunk in range(TABLE_CHUNKS):
+            span = slice(chunk * chunk_positions, (chunk + 1) * chunk_positions)
+            nc.scalar.activation(
+                out=pe_parts[:, :, :, span],
+                in_=frac[:, :, span].unsqueeze(1).to_broadcast([P, PAIR, PACK, chunk_positions]),
+                func=ACT.Sin,
+                scale=2.0 * math.pi,
+            )
+
+        w_grouped = keep.tile([P, UNITS, UNIT_COLS, PACK], BF16, align_bytes=64)
+        w_codes = keep.tile([P, UNITS, UNIT_COLS], U32, align_bytes=64)
+        w_scales = keep.tile([P, UNITS, UNIT_COLS], U8, align_bytes=64)
+
+        def transpose_w(unit):
+            words = w_rows[:, unit].bitcast(F32)
+            flipped = psum.tile([P, UNIT_BLOCKS, 2, P], F32, tag="bank")
+            for g in range(UNIT_BLOCKS):
+                for u in range(2):
+                    nc.tensor.transpose(
+                        flipped[:, g, u, :], words[:, g, u : 2 * P : 2], ident[:]
+                    )
+            return flipped
+
+        def group_w(unit):
+            nc.scalar.copy(
+                out=w_grouped[:, unit].bitcast(F32).rearrange("q (g o) u -> q g o u", g=UNIT_BLOCKS),
+                in_=flipped_w[unit][:].rearrange("q g u o -> q g o u"),
+            )
+
+        def quantise_w(unit):
+            nc.vector.quantize_mx(
+                out=w_codes[:, unit, :].bitcast(FP8X4),
+                scales=w_scales[:, unit, :],
+                in_=w_grouped[:, unit].rearrange("q c t -> q (c t)"),
+            )
+
+        tok = keep.tile([P, PAIRS, RUN, ROWS, PAIR * PACK], BF16, align_bytes=64)
+        tok_codes = keep.tile([P, PAIRS, RUN * P], U32, align_bytes=64)
+        tok_scales = keep.tile([P, PAIRS, RUN * P], U8, align_bytes=64)
+
+        def add_table(pair, chunk):
+            chunk_rows = ROWS // TABLE_CHUNKS
+            span = slice(chunk * chunk_positions, (chunk + 1) * chunk_positions)
+            rows = slice(chunk * chunk_rows, (chunk + 1) * chunk_rows)
+            nc.vector.tensor_tensor(
+                out=tok[:, pair, :, rows, :].rearrange("q r i g -> q i g r"),
+                in0=x_rows[:, pair * PAIR * PACK : (pair + 1) * PAIR * PACK, span].rearrange(
+                    "q g (i r) -> q i g r", r=RUN
+                ),
+                in1=pe[:, :, span].rearrange("q g (i r) -> q i g r", r=RUN),
+                op=ALU.add,
+            )
+
+        def quantise_tokens(pair):
+            for r in range(RUN):
+                nc.vector.quantize_mx(
+                    out=tok_codes[:, pair, r * P : (r + 1) * P].bitcast(FP8X4),
+                    scales=tok_scales[:, pair, r * P : (r + 1) * P],
+                    in_=tok[:, pair, r].rearrange("q i g -> q (i g)"),
+                )
+
+        def project(pair, unit, vector_helps):
+            stage = stage_pool.tile([P, UNIT_HEADS, RUN, HEAD_DIM], F32)
+            for half in range(2):
+                acc = psum.tile([P, 2, UNIT_COLS], F32, tag="bank")
+                for k in range(2):
+                    r = 2 * half + k
+                    nc.tensor.matmul_mx(
+                        out=acc[:, k, :],
+                        lhsT=tok_codes[:, pair, r * P : (r + 1) * P].bitcast(FP8X4),
+                        lhsT_scale=tok_scales[:, pair, r * P : (r + 1) * P],
+                        rhs=w_codes[:, unit, :].bitcast(FP8X4),
+                        rhs_scale=w_scales[:, unit, :],
+                        start=True,
+                        stop=True,
+                    )
+                by_head = acc[:].rearrange("m k (h d) -> m h k d", d=HEAD_DIM)
+                if vector_helps and half == 1:
+                    nc.vector.tensor_copy(out=stage[:, :, 2 * half : 2 * half + 2, :], in_=by_head)
+                else:
+                    nc.scalar.copy(out=stage[:, :, 2 * half : 2 * half + 2, :], in_=by_head)
+            first_head = (unit % UNITS_PER_OUTPUT) * UNIT_HEADS
+            for b in range(PAIR):
+                nc.sync.dma_start(
+                    out=outs[unit // UNITS_PER_OUTPUT][
+                        pair * PAIR + b, first_head : first_head + UNIT_HEADS
+                    ].rearrange("h (i r) d -> i h (r d)", r=RUN),
+                    in_=stage[b:P:PAIR].rearrange("m h r d -> m h (r d)"),
+                )
+
+        flipped_w = [transpose_w(unit) for unit in range(UNITS)]
+        for unit in range(COPY_AHEAD):
+            group_w(unit)
+        for chunk in range(TABLE_CHUNKS):
+            add_table(0, chunk)
+        quantise_w(0)
+        quantise_tokens(0)
+        quantise_w(1)
+        for unit in range(UNITS):
+            project(0, unit, unit % 2 == 0)
+            if unit + COPY_AHEAD < UNITS:
+                group_w(unit + COPY_AHEAD)
+            if unit + QUANTISE_AHEAD < UNITS:
+                quantise_w(unit + QUANTISE_AHEAD)
+            if unit < TABLE_CHUNKS:
+                add_table(1, unit)
+        quantise_tokens(1)
+        for unit in range(UNITS):
+            project(1, unit, True)

@@ -19,24 +19,19 @@ IMAGES = 4
 CHANNELS = 512
 POSITIONS = 256
 HEAD_DIM = 64
-BANK = 512
 
 PAIR = 2
 PAIRS = IMAGES // PAIR
 RUN = 4
 ROWS = POSITIONS // RUN
-TABLE_CHUNKS = 4
 
 UNIT_HEADS = 4
 UNIT_COLS = UNIT_HEADS * HEAD_DIM
 UNIT_BLOCKS = UNIT_COLS // P
 UNITS = 6
 UNITS_PER_OUTPUT = 2
-COPY_AHEAD = 4
-QUANTISE_AHEAD = 2
 
 RATES = CHANNELS // 2
-ROUND = 1.5 * 2.0**23
 
 FLOPS = 2 * IMAGES * POSITIONS * CHANNELS * UNITS * UNIT_COLS
 
@@ -63,98 +58,124 @@ def tile_multiheadselfattention_pa_kernel(tc, x, W_qkv, out_0, out_1, out_2):
                 ),
             )
 
-        load_x(0)
-        for unit in range(UNITS):
+        def load_w(unit):
             nc.sync.dma_start(
                 out=w_rows[:, unit],
                 in_=W_qkv[unit * UNIT_COLS : (unit + 1) * UNIT_COLS, :].rearrange(
-                    "(g o) c -> o g c", o=P
+                    "(o g) c -> o g c", o=P
                 ),
             )
-        load_x(1)
 
-        chan_int = keep.tile([P, PACK], I32)
+        load_w(0)
+        load_x(0)
+        load_w(1)
+        load_w(2)
+        load_x(1)
+        load_w(3)
+        load_w(4)
+        load_w(5)
+
+        chan = keep.tile([P, PACK], F32)
         for first in (0, HALF_P):
             nc.gpsimd.iota(
-                chan_int[first : first + HALF_P], pattern=[[1, PACK]], base=0, channel_multiplier=PACK
+                chan[first : first + HALF_P],
+                pattern=[[1, PACK]],
+                base=0,
+                channel_multiplier=PACK,
+                allow_small_or_imprecise_dtypes=True,
             )
+        exponent = keep.tile([P, PACK], F32)
+        nc.gpsimd.tensor_scalar(
+            out=exponent[:], in0=chan[:], scalar1=-1.0 / RATES, scalar2=None, op0=ALU.mult
+        )
         base = keep.tile([P, PACK], F32)
         nc.gpsimd.memset(base[:], 10000.0)
-        exponent = keep.tile([P, PACK], F32)
-        nc.vector.tensor_scalar_mul(out=exponent[:], in0=chan_int[:], scalar1=-1.0 / RATES)
         rate = keep.tile([P, PACK], F32)
         nc.gpsimd.tensor_tensor(out=rate[:], in0=base[:], in1=exponent[:], op=ALU.pow)
-        own_index = keep.tile([P, 1], I32)
-        nc.gpsimd.iota(own_index[:], pattern=[[1, 1]], base=0, channel_multiplier=1)
-        phase = keep.tile([P, 1], F32)
-        nc.vector.memset(phase[0:HALF_P], 0.0)
-        nc.vector.memset(phase[HALF_P:P], 0.25)
-
-        warm = keep.tile([P, 2], F32)
-        nc.vector.memset(warm[:, 0:1], 0.0)
-        nc.scalar.activation(out=warm[:, 1:2], in_=warm[:, 0:1], func=ACT.Sin)
+        index = keep.tile([P, 1], F32)
+        nc.gpsimd.iota(
+            index[:],
+            pattern=[[1, 1]],
+            base=0,
+            channel_multiplier=1,
+            allow_small_or_imprecise_dtypes=True,
+        )
 
         ones = keep.tile([P, POSITIONS], F32)
         nc.vector.memset(ones[:], 1.0)
+        warm = keep.tile([P, 2], F32)
+        nc.vector.memset(warm[:, 0:1], 0.0)
+        nc.scalar.activation(out=warm[:, 1:2], in_=warm[:, 0:1], func=ACT.Sin)
         count = keep.tile([P, POSITIONS], F32)
         nc.vector.tensor_tensor_scan(
             out=count[:], data0=ones[:], data1=ones[:], initial=-1.0, op0=ALU.mult, op1=ALU.add
         )
+        phase = keep.tile([P, 1], F32)
+        nc.vector.memset(phase[0:HALF_P], 0.0)
+        nc.vector.memset(phase[HALF_P:P], 0.25)
+        count_turns = keep.tile([P, POSITIONS], F32)
+        nc.vector.tensor_scalar_mul(out=count_turns[:], in0=count[:], scalar1=1.0 / (2.0 * math.pi))
+        phase_angle = keep.tile([P, 1], F32)
+        nc.vector.tensor_scalar_mul(out=phase_angle[:], in0=phase[:], scalar1=2.0 * math.pi)
 
-        turn_rate = keep.tile([P, PACK], F32)
-        nc.vector.tensor_scalar_mul(out=turn_rate[:], in0=rate[:], scalar1=1.0 / (2.0 * math.pi))
-        turns = keep.tile([P, PACK, POSITIONS], F32)
-        for t in range(PACK):
+        whole = keep.tile([P, PACK, POSITIONS], I32)
+        frac = keep.tile([P, PACK, POSITIONS], F32)
+        pe = keep.tile([P, PACK, POSITIONS], F32)
+
+        def whole_turns(t):
             nc.vector.tensor_scalar(
-                out=turns[:, t, :],
-                in0=count[:],
-                scalar1=turn_rate[:, t : t + 1],
+                out=whole[:, t, :],
+                in0=count_turns[:],
+                scalar1=rate[:, t : t + 1],
                 scalar2=phase[:],
                 op0=ALU.mult,
                 op1=ALU.add,
             )
-        whole = keep.tile([P, PACK, POSITIONS], F32)
-        nc.vector.tensor_scalar(
-            out=whole[:], in0=turns[:], scalar1=ROUND, scalar2=ROUND, op0=ALU.add, op1=ALU.subtract
-        )
-        frac = keep.tile([P, PACK, POSITIONS], F32)
-        nc.vector.tensor_tensor(out=frac[:], in0=turns[:], in1=whole[:], op=ALU.subtract)
-        index = keep.tile([P, 1], F32)
-        nc.vector.tensor_copy(out=index[:], in_=own_index[:])
+
+        def take_away(t):
+            nc.vector.scalar_tensor_tensor(
+                out=frac[:, t, :],
+                in0=count_turns[:],
+                scalar=rate[:, t : t + 1],
+                in1=whole[:, t, :],
+                op0=ALU.mult,
+                op1=ALU.subtract,
+            )
+            nc.scalar.activation(
+                out=pe[:, t, :],
+                in_=frac[:, t, :],
+                func=ACT.Sin,
+                scale=2.0 * math.pi,
+                bias=phase_angle[:],
+            )
+
+        whole_turns(0)
+        for t in range(PACK):
+            if t + 1 < PACK:
+                whole_turns(t + 1)
+            take_away(t)
         ident = keep.tile([P, P], F32)
         nc.vector.tensor_scalar(
             out=ident[:], in0=count[:, 0:P], scalar1=index[:], scalar2=None, op0=ALU.is_equal
         )
-        pe = keep.tile([P, PAIR * PACK, POSITIONS], F32)
-        pe_parts = pe[:].rearrange("q (b t) n -> q b t n", b=PAIR)
-        chunk_positions = POSITIONS // TABLE_CHUNKS
-        for chunk in range(TABLE_CHUNKS):
-            span = slice(chunk * chunk_positions, (chunk + 1) * chunk_positions)
-            nc.scalar.activation(
-                out=pe_parts[:, :, :, span],
-                in_=frac[:, :, span].unsqueeze(1).to_broadcast([P, PAIR, PACK, chunk_positions]),
-                func=ACT.Sin,
-                scale=2.0 * math.pi,
-            )
 
         w_grouped = keep.tile([P, UNITS, UNIT_COLS, PACK], BF16, align_bytes=64)
         w_codes = keep.tile([P, UNITS, UNIT_COLS], U32, align_bytes=64)
         w_scales = keep.tile([P, UNITS, UNIT_COLS], U8, align_bytes=64)
+        flipped_w = {}
 
         def transpose_w(unit):
             words = w_rows[:, unit].bitcast(F32)
             flipped = psum.tile([P, UNIT_BLOCKS, 2, P], F32, tag="bank")
             for g in range(UNIT_BLOCKS):
                 for u in range(2):
-                    nc.tensor.transpose(
-                        flipped[:, g, u, :], words[:, g, u : 2 * P : 2], ident[:]
-                    )
-            return flipped
+                    nc.tensor.transpose(flipped[:, g, u, :], words[:, g, u : 2 * P : 2], ident[:])
+            flipped_w[unit] = flipped
 
         def group_w(unit):
             nc.scalar.copy(
-                out=w_grouped[:, unit].bitcast(F32).rearrange("q (g o) u -> q g o u", g=UNIT_BLOCKS),
-                in_=flipped_w[unit][:].rearrange("q g u o -> q g o u"),
+                out=w_grouped[:, unit].bitcast(F32).rearrange("q (o g) u -> q o g u", g=UNIT_BLOCKS),
+                in_=flipped_w[unit][:].rearrange("q g u o -> q o g u"),
             )
 
         def quantise_w(unit):
@@ -168,26 +189,25 @@ def tile_multiheadselfattention_pa_kernel(tc, x, W_qkv, out_0, out_1, out_2):
         tok_codes = keep.tile([P, PAIRS, RUN * P], U32, align_bytes=64)
         tok_scales = keep.tile([P, PAIRS, RUN * P], U8, align_bytes=64)
 
-        def add_table(pair, chunk):
-            chunk_rows = ROWS // TABLE_CHUNKS
-            span = slice(chunk * chunk_positions, (chunk + 1) * chunk_positions)
-            rows = slice(chunk * chunk_rows, (chunk + 1) * chunk_rows)
+        def add_table(pair, r):
             nc.vector.tensor_tensor(
-                out=tok[:, pair, :, rows, :].rearrange("q r i g -> q i g r"),
-                in0=x_rows[:, pair * PAIR * PACK : (pair + 1) * PAIR * PACK, span].rearrange(
-                    "q g (i r) -> q i g r", r=RUN
-                ),
-                in1=pe[:, :, span].rearrange("q g (i r) -> q i g r", r=RUN),
+                out=tok[:, pair, r].rearrange("q i (b t) -> q i b t", b=PAIR),
+                in0=x_rows[:, pair * PAIR * PACK : (pair + 1) * PAIR * PACK, :].rearrange(
+                    "q (b t) (i r) -> q r i b t", b=PAIR, r=RUN
+                )[:, r],
+                in1=pe[:]
+                .rearrange("q t (i r) -> q r i t", r=RUN)[:, r]
+                .unsqueeze(2)
+                .to_broadcast([P, ROWS, PAIR, PACK]),
                 op=ALU.add,
             )
 
-        def quantise_tokens(pair):
-            for r in range(RUN):
-                nc.vector.quantize_mx(
-                    out=tok_codes[:, pair, r * P : (r + 1) * P].bitcast(FP8X4),
-                    scales=tok_scales[:, pair, r * P : (r + 1) * P],
-                    in_=tok[:, pair, r].rearrange("q i g -> q (i g)"),
-                )
+        def quantise_tokens(pair, r):
+            nc.vector.quantize_mx(
+                out=tok_codes[:, pair, r * P : (r + 1) * P].bitcast(FP8X4),
+                scales=tok_scales[:, pair, r * P : (r + 1) * P],
+                in_=tok[:, pair, r].rearrange("q i g -> q (i g)"),
+            )
 
         def project(pair, unit, vector_helps):
             stage = stage_pool.tile([P, UNIT_HEADS, RUN, HEAD_DIM], F32)
@@ -218,22 +238,29 @@ def tile_multiheadselfattention_pa_kernel(tc, x, W_qkv, out_0, out_1, out_2):
                     in_=stage[b:P:PAIR].rearrange("m h r d -> m h (r d)"),
                 )
 
-        flipped_w = [transpose_w(unit) for unit in range(UNITS)]
-        for unit in range(COPY_AHEAD):
-            group_w(unit)
-        for chunk in range(TABLE_CHUNKS):
-            add_table(0, chunk)
+        transpose_w(0)
+        group_w(0)
+        transpose_w(1)
+        group_w(1)
+        add_table(0, 0)
+        add_table(0, 1)
         quantise_w(0)
-        quantise_tokens(0)
+        quantise_tokens(0, 0)
+        add_table(0, 2)
+        quantise_tokens(0, 1)
+        add_table(0, 3)
+        quantise_tokens(0, 2)
         quantise_w(1)
+        quantise_tokens(0, 3)
         for unit in range(UNITS):
-            project(0, unit, unit % 2 == 0)
-            if unit + COPY_AHEAD < UNITS:
-                group_w(unit + COPY_AHEAD)
-            if unit + QUANTISE_AHEAD < UNITS:
-                quantise_w(unit + QUANTISE_AHEAD)
-            if unit < TABLE_CHUNKS:
-                add_table(1, unit)
-        quantise_tokens(1)
+            project(0, unit, unit > 0)
+            if unit + 2 < UNITS:
+                transpose_w(unit + 2)
+                group_w(unit + 2)
+                quantise_w(unit + 2)
+            if 1 <= unit <= RUN:
+                add_table(1, unit - 1)
+        for r in range(RUN):
+            quantise_tokens(1, r)
         for unit in range(UNITS):
             project(1, unit, True)

@@ -24,6 +24,7 @@ PAIR = 2
 PAIRS = IMAGES // PAIR
 RUN = 4
 ROWS = POSITIONS // RUN
+NEAR = 4
 
 UNIT_HEADS = 4
 UNIT_COLS = UNIT_HEADS * HEAD_DIM
@@ -66,8 +67,8 @@ def tile_multiheadselfattention_pa_kernel(tc, x, W_qkv, out_0, out_1, out_2):
                 ),
             )
 
-        load_w(0)
         load_x(0)
+        load_w(0)
         load_w(1)
         load_w(2)
         load_x(1)
@@ -75,88 +76,97 @@ def tile_multiheadselfattention_pa_kernel(tc, x, W_qkv, out_0, out_1, out_2):
         load_w(4)
         load_w(5)
 
-        chan = keep.tile([P, PACK], F32)
-        for first in (0, HALF_P):
+        def iota(tile, pattern, channel_multiplier):
             nc.gpsimd.iota(
-                chan[first : first + HALF_P],
-                pattern=[[1, PACK]],
+                tile,
+                pattern=pattern,
                 base=0,
-                channel_multiplier=PACK,
+                channel_multiplier=channel_multiplier,
                 allow_small_or_imprecise_dtypes=True,
             )
-        exponent = keep.tile([P, PACK], F32)
+
+        position = keep.tile([P, RUN, ROWS], F32)
+        iota(position[:], [[1, RUN], [RUN, ROWS]], 0)
+        chan = keep.tile([P, 1], F32)
+        iota(chan[:], [[1, 1]], PACK)
+        base = keep.tile([P, 1], F32)
+        nc.vector.memset(base[:], 10000.0)
+        cosine = keep.tile([P, 1], F32)
+        nc.vector.memset(cosine[0:HALF_P], 0.0)
+        nc.vector.memset(cosine[HALF_P:P], 1.0)
+        exponent = keep.tile([P, 1], F32)
         nc.gpsimd.tensor_scalar(
-            out=exponent[:], in0=chan[:], scalar1=-1.0 / RATES, scalar2=None, op0=ALU.mult
+            out=exponent[:],
+            in0=chan[:],
+            scalar1=-1.0 / RATES,
+            scalar2=cosine[:],
+            op0=ALU.mult,
+            op1=ALU.add,
         )
-        base = keep.tile([P, PACK], F32)
-        nc.gpsimd.memset(base[:], 10000.0)
-        rate = keep.tile([P, PACK], F32)
+        rate = keep.tile([P, 1], F32)
         nc.gpsimd.tensor_tensor(out=rate[:], in0=base[:], in1=exponent[:], op=ALU.pow)
         index = keep.tile([P, 1], F32)
-        nc.gpsimd.iota(
-            index[:],
-            pattern=[[1, 1]],
-            base=0,
-            channel_multiplier=1,
-            allow_small_or_imprecise_dtypes=True,
-        )
+        iota(index[:], [[1, 1]], 1)
+        column = keep.tile([P, P], F32)
+        iota(column[:], [[1, P]], 0)
 
-        ones = keep.tile([P, POSITIONS], F32)
-        nc.vector.memset(ones[:], 1.0)
         warm = keep.tile([P, 2], F32)
         nc.vector.memset(warm[:, 0:1], 0.0)
         nc.scalar.activation(out=warm[:, 1:2], in_=warm[:, 0:1], func=ACT.Sin)
-        count = keep.tile([P, POSITIONS], F32)
-        nc.vector.tensor_tensor_scan(
-            out=count[:], data0=ones[:], data1=ones[:], initial=-1.0, op0=ALU.mult, op1=ALU.add
-        )
         phase = keep.tile([P, 1], F32)
-        nc.vector.memset(phase[0:HALF_P], 0.0)
-        nc.vector.memset(phase[HALF_P:P], 0.25)
-        count_turns = keep.tile([P, POSITIONS], F32)
-        nc.vector.tensor_scalar_mul(out=count_turns[:], in0=count[:], scalar1=1.0 / (2.0 * math.pi))
+        nc.vector.tensor_scalar_mul(out=phase[:], in0=cosine[:], scalar1=0.25)
         phase_angle = keep.tile([P, 1], F32)
-        nc.vector.tensor_scalar_mul(out=phase_angle[:], in0=phase[:], scalar1=2.0 * math.pi)
+        nc.vector.tensor_scalar_mul(out=phase_angle[:], in0=cosine[:], scalar1=0.5 * math.pi)
+        steps = keep.tile([P, RUN, PACK, ROWS], F32)
+        for t in range(PACK):
+            nc.vector.tensor_scalar_mul(
+                out=steps[:, :, t, :],
+                in0=position[:],
+                scalar1=10000.0 ** (-t / RATES) / (2.0 * math.pi),
+            )
 
-        whole = keep.tile([P, PACK, POSITIONS], I32)
-        frac = keep.tile([P, PACK, POSITIONS], F32)
-        pe = keep.tile([P, PACK, POSITIONS], F32)
+        whole = keep.tile([P, RUN, PACK, ROWS], I32)
+        frac = keep.tile([P, RUN, PACK, ROWS], F32)
+        pe = keep.tile([P, RUN, PAIR * PACK, ROWS], F32)
 
-        def whole_turns(t):
+        def whole_turns(r):
             nc.vector.tensor_scalar(
-                out=whole[:, t, :],
-                in0=count_turns[:],
-                scalar1=rate[:, t : t + 1],
+                out=whole[:, r].rearrange("q t i -> q (t i)"),
+                in0=steps[:, r].rearrange("q t i -> q (t i)"),
+                scalar1=rate[:],
                 scalar2=phase[:],
                 op0=ALU.mult,
                 op1=ALU.add,
             )
 
-        def take_away(t):
+        def take_away(r):
             nc.vector.scalar_tensor_tensor(
-                out=frac[:, t, :],
-                in0=count_turns[:],
-                scalar=rate[:, t : t + 1],
-                in1=whole[:, t, :],
+                out=frac[:, r].rearrange("q t i -> q (t i)"),
+                in0=steps[:, r].rearrange("q t i -> q (t i)"),
+                scalar=rate[:],
+                in1=whole[:, r].rearrange("q t i -> q (t i)"),
                 op0=ALU.mult,
                 op1=ALU.subtract,
             )
             nc.scalar.activation(
-                out=pe[:, t, :],
-                in_=frac[:, t, :],
+                out=pe[:, r].rearrange("q (b t) i -> q b (t i)", b=PAIR),
+                in_=frac[:, r]
+                .rearrange("q t i -> q (t i)")
+                .unsqueeze(1)
+                .to_broadcast([P, PAIR, PACK * ROWS]),
                 func=ACT.Sin,
                 scale=2.0 * math.pi,
                 bias=phase_angle[:],
             )
 
         whole_turns(0)
-        for t in range(PACK):
-            if t + 1 < PACK:
-                whole_turns(t + 1)
-            take_away(t)
+        for r in range(RUN):
+            if r + 1 < RUN:
+                whole_turns(r + 1)
+            take_away(r)
         ident = keep.tile([P, P], F32)
         nc.vector.tensor_scalar(
-            out=ident[:], in0=count[:, 0:P], scalar1=index[:], scalar2=None, op0=ALU.is_equal
+            out=ident[:], in0=column[:], scalar1=index[:], scalar2=None, op0=ALU.is_equal
         )
 
         w_grouped = keep.tile([P, UNITS, UNIT_COLS, PACK], BF16, align_bytes=64)
@@ -191,14 +201,11 @@ def tile_multiheadselfattention_pa_kernel(tc, x, W_qkv, out_0, out_1, out_2):
 
         def add_table(pair, r):
             nc.vector.tensor_tensor(
-                out=tok[:, pair, r].rearrange("q i (b t) -> q i b t", b=PAIR),
+                out=tok[:, pair, r].rearrange("q (j n) g -> q j g n", n=NEAR),
                 in0=x_rows[:, pair * PAIR * PACK : (pair + 1) * PAIR * PACK, :].rearrange(
-                    "q (b t) (i r) -> q r i b t", b=PAIR, r=RUN
+                    "q g (j n r) -> q r j g n", n=NEAR, r=RUN
                 )[:, r],
-                in1=pe[:]
-                .rearrange("q t (i r) -> q r i t", r=RUN)[:, r]
-                .unsqueeze(2)
-                .to_broadcast([P, ROWS, PAIR, PACK]),
+                in1=pe[:, r].rearrange("q g (j n) -> q j g n", n=NEAR),
                 op=ALU.add,
             )
 
@@ -209,7 +216,7 @@ def tile_multiheadselfattention_pa_kernel(tc, x, W_qkv, out_0, out_1, out_2):
                 in_=tok[:, pair, r].rearrange("q i g -> q (i g)"),
             )
 
-        def project(pair, unit, vector_helps):
+        def project(pair, unit):
             stage = stage_pool.tile([P, UNIT_HEADS, RUN, HEAD_DIM], F32)
             for half in range(2):
                 acc = psum.tile([P, 2, UNIT_COLS], F32, tag="bank")
@@ -225,7 +232,7 @@ def tile_multiheadselfattention_pa_kernel(tc, x, W_qkv, out_0, out_1, out_2):
                         stop=True,
                     )
                 by_head = acc[:].rearrange("m k (h d) -> m h k d", d=HEAD_DIM)
-                if vector_helps and half == 1:
+                if half == 1:
                     nc.vector.tensor_copy(out=stage[:, :, 2 * half : 2 * half + 2, :], in_=by_head)
                 else:
                     nc.scalar.copy(out=stage[:, :, 2 * half : 2 * half + 2, :], in_=by_head)
@@ -244,23 +251,24 @@ def tile_multiheadselfattention_pa_kernel(tc, x, W_qkv, out_0, out_1, out_2):
         group_w(1)
         add_table(0, 0)
         add_table(0, 1)
-        quantise_w(0)
         quantise_tokens(0, 0)
+        quantise_w(0)
         add_table(0, 2)
         quantise_tokens(0, 1)
         add_table(0, 3)
         quantise_tokens(0, 2)
-        quantise_w(1)
         quantise_tokens(0, 3)
+        quantise_w(1)
         for unit in range(UNITS):
-            project(0, unit, unit > 0)
+            project(0, unit)
             if unit + 2 < UNITS:
                 transpose_w(unit + 2)
                 group_w(unit + 2)
-                quantise_w(unit + 2)
+            if unit < RUN:
+                add_table(1, unit)
             if 1 <= unit <= RUN:
-                add_table(1, unit - 1)
-        for r in range(RUN):
-            quantise_tokens(1, r)
+                quantise_tokens(1, unit - 1)
+            if unit + 2 < UNITS:
+                quantise_w(unit + 2)
         for unit in range(UNITS):
-            project(1, unit, True)
+            project(1, unit)

@@ -42,7 +42,7 @@ def tile_multiheadselfattention_pa_kernel(tc, x, W_qkv, out_0, out_1, out_2):
     outs = (out_0, out_1, out_2)
     with ExitStack() as pools:
         keep = pools.enter_context(tc.tile_pool(name="keep", bufs=1))
-        stage_pool = pools.enter_context(tc.tile_pool(name="stage", bufs=6))
+        stage_pool = pools.enter_context(tc.tile_pool(name="stage", bufs=12))
         psum = pools.enter_context(tc.psum_pool(name="psum", bufs=8))
         pools.enter_context(tc.manual_schedule())
 
@@ -216,59 +216,85 @@ def tile_multiheadselfattention_pa_kernel(tc, x, W_qkv, out_0, out_1, out_2):
                 in_=tok[:, pair, r].rearrange("q i g -> q (i g)"),
             )
 
-        def project(pair, unit):
-            stage = stage_pool.tile([P, UNIT_HEADS, RUN, HEAD_DIM], F32)
-            for half in range(2):
-                acc = psum.tile([P, 2, UNIT_COLS], F32, tag="bank")
-                for k in range(2):
-                    r = 2 * half + k
-                    nc.tensor.matmul_mx(
-                        out=acc[:, k, :],
-                        lhsT=tok_codes[:, pair, r * P : (r + 1) * P].bitcast(FP8X4),
-                        lhsT_scale=tok_scales[:, pair, r * P : (r + 1) * P],
-                        rhs=w_codes[:, unit, :].bitcast(FP8X4),
-                        rhs_scale=w_scales[:, unit, :],
-                        start=True,
-                        stop=True,
-                    )
-                by_head = acc[:].rearrange("m k (h d) -> m h k d", d=HEAD_DIM)
-                if half == 1:
-                    nc.vector.tensor_copy(out=stage[:, :, 2 * half : 2 * half + 2, :], in_=by_head)
-                else:
-                    nc.scalar.copy(out=stage[:, :, 2 * half : 2 * half + 2, :], in_=by_head)
+        def multiply(pair, unit, half):
+            acc = psum.tile([P, 2, UNIT_COLS], F32, tag="bank")
+            for k in range(2):
+                r = 2 * half + k
+                nc.tensor.matmul_mx(
+                    out=acc[:, k, :],
+                    lhsT=tok_codes[:, pair, r * P : (r + 1) * P].bitcast(FP8X4),
+                    lhsT_scale=tok_scales[:, pair, r * P : (r + 1) * P],
+                    rhs=w_codes[:, unit, :].bitcast(FP8X4),
+                    rhs_scale=w_scales[:, unit, :],
+                    start=True,
+                    stop=True,
+                )
+            return acc[:].rearrange("m k (h d) -> m h k d", d=HEAD_DIM)
+
+        def store(pair, unit, stage, first, last):
             first_head = (unit % UNITS_PER_OUTPUT) * UNIT_HEADS
             for b in range(PAIR):
                 nc.sync.dma_start(
                     out=outs[unit // UNITS_PER_OUTPUT][
                         pair * PAIR + b, first_head : first_head + UNIT_HEADS
-                    ].rearrange("h (i r) d -> i h (r d)", r=RUN),
-                    in_=stage[b:P:PAIR].rearrange("m h r d -> m h (r d)"),
+                    ].rearrange("h (i r) d -> i h r d", r=RUN)[:, :, first:last, :]
+                    .rearrange("i h r d -> i h (r d)"),
+                    in_=stage[b:P:PAIR, :, first:last, :].rearrange("m h r d -> m h (r d)"),
                 )
 
-        transpose_w(0)
-        group_w(0)
-        transpose_w(1)
-        group_w(1)
+        def project(pair, unit, vector_helps):
+            stage = stage_pool.tile([P, UNIT_HEADS, RUN, HEAD_DIM], F32)
+            for half in range(2):
+                by_head = multiply(pair, unit, half)
+                copy = nc.vector.tensor_copy if vector_helps and half == 1 else nc.scalar.copy
+                copy(out=stage[:, :, 2 * half : 2 * half + 2, :], in_=by_head)
+            store(pair, unit, stage, 0, RUN)
+
+        def prepare_w(unit):
+            transpose_w(unit)
+            group_w(unit)
+
+        prepare_w(0)
+        prepare_w(1)
         add_table(0, 0)
         add_table(0, 1)
         quantise_tokens(0, 0)
-        quantise_w(0)
-        add_table(0, 2)
         quantise_tokens(0, 1)
+        add_table(0, 2)
+        quantise_w(0)
         add_table(0, 3)
         quantise_tokens(0, 2)
         quantise_tokens(0, 3)
+        stage = stage_pool.tile([P, UNIT_HEADS, RUN, HEAD_DIM], F32)
+        by_head = multiply(0, 0, 0)
+        nc.scalar.copy(out=stage[:, :, 0:2, :], in_=by_head)
+        store(0, 0, stage, 0, 2)
+        prepare_w(2)
+        by_head = multiply(0, 0, 1)
         quantise_w(1)
-        for unit in range(UNITS):
-            project(0, unit)
-            if unit + 2 < UNITS:
-                transpose_w(unit + 2)
-                group_w(unit + 2)
-            if unit < RUN:
-                add_table(1, unit)
-            if 1 <= unit <= RUN:
-                quantise_tokens(1, unit - 1)
-            if unit + 2 < UNITS:
-                quantise_w(unit + 2)
-        for unit in range(UNITS):
-            project(1, unit)
+        nc.vector.tensor_copy(out=stage[:, :, 2:4, :], in_=by_head)
+        store(0, 0, stage, 2, 4)
+        project(0, 1, True)
+        quantise_w(2)
+        add_table(1, 0)
+        prepare_w(3)
+        project(0, 2, False)
+        quantise_w(3)
+        add_table(1, 1)
+        quantise_tokens(1, 0)
+        prepare_w(4)
+        project(0, 3, True)
+        quantise_w(4)
+        add_table(1, 2)
+        quantise_tokens(1, 1)
+        project(0, 4, False)
+        add_table(1, 3)
+        quantise_tokens(1, 2)
+        quantise_tokens(1, 3)
+        for unit in range(UNITS - 1):
+            project(1, unit, True)
+            if unit == 0:
+                prepare_w(UNITS - 1)
+                quantise_w(UNITS - 1)
+        for pair in range(PAIRS):
+            project(pair, UNITS - 1, True)

@@ -24,7 +24,9 @@ PAIR = 2
 PAIRS = IMAGES // PAIR
 RUN = 4
 ROWS = POSITIONS // RUN
-NEAR = 4
+TABLE_CHUNKS = 4
+CHUNK = POSITIONS // TABLE_CHUNKS
+CHUNK_ROWS = ROWS // TABLE_CHUNKS
 
 UNIT_HEADS = 4
 UNIT_COLS = UNIT_HEADS * HEAD_DIM
@@ -85,8 +87,8 @@ def tile_multiheadselfattention_pa_kernel(tc, x, W_qkv, out_0, out_1, out_2):
                 allow_small_or_imprecise_dtypes=True,
             )
 
-        position = keep.tile([P, RUN, ROWS], F32)
-        iota(position[:], [[1, RUN], [RUN, ROWS]], 0)
+        position = keep.tile([P, TABLE_CHUNKS, CHUNK], F32)
+        iota(position[:], [[CHUNK, TABLE_CHUNKS], [1, CHUNK]], 0)
         chan = keep.tile([P, 1], F32)
         iota(chan[:], [[1, 1]], PACK)
         base = keep.tile([P, 1], F32)
@@ -107,8 +109,6 @@ def tile_multiheadselfattention_pa_kernel(tc, x, W_qkv, out_0, out_1, out_2):
         nc.gpsimd.tensor_tensor(out=rate[:], in0=base[:], in1=exponent[:], op=ALU.pow)
         index = keep.tile([P, 1], F32)
         iota(index[:], [[1, 1]], 1)
-        column = keep.tile([P, P], F32)
-        iota(column[:], [[1, P]], 0)
 
         warm = keep.tile([P, 2], F32)
         nc.vector.memset(warm[:, 0:1], 0.0)
@@ -117,7 +117,7 @@ def tile_multiheadselfattention_pa_kernel(tc, x, W_qkv, out_0, out_1, out_2):
         nc.vector.tensor_scalar_mul(out=phase[:], in0=cosine[:], scalar1=0.25)
         phase_angle = keep.tile([P, 1], F32)
         nc.vector.tensor_scalar_mul(out=phase_angle[:], in0=cosine[:], scalar1=0.5 * math.pi)
-        steps = keep.tile([P, RUN, PACK, ROWS], F32)
+        steps = keep.tile([P, TABLE_CHUNKS, PACK, CHUNK], F32)
         for t in range(PACK):
             nc.vector.tensor_scalar_mul(
                 out=steps[:, :, t, :],
@@ -125,48 +125,51 @@ def tile_multiheadselfattention_pa_kernel(tc, x, W_qkv, out_0, out_1, out_2):
                 scalar1=10000.0 ** (-t / RATES) / (2.0 * math.pi),
             )
 
-        whole = keep.tile([P, RUN, PACK, ROWS], I32)
-        frac = keep.tile([P, RUN, PACK, ROWS], F32)
-        pe = keep.tile([P, RUN, PAIR * PACK, ROWS], F32)
+        whole = keep.tile([P, TABLE_CHUNKS, PACK, CHUNK], I32)
+        frac = keep.tile([P, TABLE_CHUNKS, PACK, CHUNK], F32)
+        pe = keep.tile([P, PAIR * PACK, POSITIONS], F32)
 
-        def whole_turns(r):
+        def whole_turns(chunk):
             nc.vector.tensor_scalar(
-                out=whole[:, r].rearrange("q t i -> q (t i)"),
-                in0=steps[:, r].rearrange("q t i -> q (t i)"),
+                out=whole[:, chunk].rearrange("q t n -> q (t n)"),
+                in0=steps[:, chunk].rearrange("q t n -> q (t n)"),
                 scalar1=rate[:],
                 scalar2=phase[:],
                 op0=ALU.mult,
                 op1=ALU.add,
             )
 
-        def take_away(r):
+        def take_away(chunk):
             nc.vector.scalar_tensor_tensor(
-                out=frac[:, r].rearrange("q t i -> q (t i)"),
-                in0=steps[:, r].rearrange("q t i -> q (t i)"),
+                out=frac[:, chunk].rearrange("q t n -> q (t n)"),
+                in0=steps[:, chunk].rearrange("q t n -> q (t n)"),
                 scalar=rate[:],
-                in1=whole[:, r].rearrange("q t i -> q (t i)"),
+                in1=whole[:, chunk].rearrange("q t n -> q (t n)"),
                 op0=ALU.mult,
                 op1=ALU.subtract,
             )
             nc.scalar.activation(
-                out=pe[:, r].rearrange("q (b t) i -> q b (t i)", b=PAIR),
-                in_=frac[:, r]
-                .rearrange("q t i -> q (t i)")
-                .unsqueeze(1)
-                .to_broadcast([P, PAIR, PACK * ROWS]),
+                out=pe[:, :, chunk * CHUNK : (chunk + 1) * CHUNK].rearrange(
+                    "q (b t) n -> q b t n", b=PAIR
+                ),
+                in_=frac[:, chunk].unsqueeze(1).to_broadcast([P, PAIR, PACK, CHUNK]),
                 func=ACT.Sin,
                 scale=2.0 * math.pi,
                 bias=phase_angle[:],
             )
 
         whole_turns(0)
-        for r in range(RUN):
-            if r + 1 < RUN:
-                whole_turns(r + 1)
-            take_away(r)
+        for chunk in range(TABLE_CHUNKS):
+            if chunk + 1 < TABLE_CHUNKS:
+                whole_turns(chunk + 1)
+            take_away(chunk)
         ident = keep.tile([P, P], F32)
         nc.vector.tensor_scalar(
-            out=ident[:], in0=column[:], scalar1=index[:], scalar2=None, op0=ALU.is_equal
+            out=ident[:],
+            in0=position[:].rearrange("q c n -> q (c n)")[:, 0:P],
+            scalar1=index[:],
+            scalar2=None,
+            op0=ALU.is_equal,
         )
 
         w_grouped = keep.tile([P, UNITS, UNIT_COLS, PACK], BF16, align_bytes=64)
@@ -199,13 +202,15 @@ def tile_multiheadselfattention_pa_kernel(tc, x, W_qkv, out_0, out_1, out_2):
         tok_codes = keep.tile([P, PAIRS, RUN * P], U32, align_bytes=64)
         tok_scales = keep.tile([P, PAIRS, RUN * P], U8, align_bytes=64)
 
-        def add_table(pair, r):
+        def add_table(pair, chunk):
+            span = slice(chunk * CHUNK, (chunk + 1) * CHUNK)
+            rows = slice(chunk * CHUNK_ROWS, (chunk + 1) * CHUNK_ROWS)
             nc.vector.tensor_tensor(
-                out=tok[:, pair, r].rearrange("q (j n) g -> q j g n", n=NEAR),
-                in0=x_rows[:, pair * PAIR * PACK : (pair + 1) * PAIR * PACK, :].rearrange(
-                    "q g (j n r) -> q r j g n", n=NEAR, r=RUN
-                )[:, r],
-                in1=pe[:, r].rearrange("q g (j n) -> q j g n", n=NEAR),
+                out=tok[:, pair, :, rows, :].rearrange("q r i g -> q i g r"),
+                in0=x_rows[:, pair * PAIR * PACK : (pair + 1) * PAIR * PACK, span].rearrange(
+                    "q g (i r) -> q i g r", r=RUN
+                ),
+                in1=pe[:, :, span].rearrange("q g (i r) -> q i g r", r=RUN),
                 op=ALU.add,
             )
 
@@ -256,24 +261,14 @@ def tile_multiheadselfattention_pa_kernel(tc, x, W_qkv, out_0, out_1, out_2):
 
         prepare_w(0)
         prepare_w(1)
-        add_table(0, 0)
-        add_table(0, 1)
-        quantise_tokens(0, 0)
-        quantise_tokens(0, 1)
-        add_table(0, 2)
+        for chunk in range(TABLE_CHUNKS):
+            add_table(0, chunk)
         quantise_w(0)
-        add_table(0, 3)
-        quantise_tokens(0, 2)
-        quantise_tokens(0, 3)
-        stage = stage_pool.tile([P, UNIT_HEADS, RUN, HEAD_DIM], F32)
-        by_head = multiply(0, 0, 0)
-        nc.scalar.copy(out=stage[:, :, 0:2, :], in_=by_head)
-        store(0, 0, stage, 0, 2)
-        prepare_w(2)
-        by_head = multiply(0, 0, 1)
+        for r in range(RUN):
+            quantise_tokens(0, r)
         quantise_w(1)
-        nc.vector.tensor_copy(out=stage[:, :, 2:4, :], in_=by_head)
-        store(0, 0, stage, 2, 4)
+        project(0, 0, True)
+        prepare_w(2)
         project(0, 1, True)
         quantise_w(2)
         add_table(1, 0)
@@ -281,16 +276,14 @@ def tile_multiheadselfattention_pa_kernel(tc, x, W_qkv, out_0, out_1, out_2):
         project(0, 2, False)
         quantise_w(3)
         add_table(1, 1)
-        quantise_tokens(1, 0)
         prepare_w(4)
         project(0, 3, True)
         quantise_w(4)
         add_table(1, 2)
-        quantise_tokens(1, 1)
         project(0, 4, False)
         add_table(1, 3)
-        quantise_tokens(1, 2)
-        quantise_tokens(1, 3)
+        for r in range(RUN):
+            quantise_tokens(1, r)
         for unit in range(UNITS - 1):
             project(1, unit, True)
             if unit == 0:

@@ -73,8 +73,8 @@ def tile_multiheadselfattention_pa_kernel(tc, x, W_qkv, out_0, out_1, out_2):
         load_w(0)
         load_w(1)
         load_w(2)
-        load_x(1)
         load_w(3)
+        load_x(1)
         load_w(4)
         load_w(5)
 
@@ -255,39 +255,25 @@ def tile_multiheadselfattention_pa_kernel(tc, x, W_qkv, out_0, out_1, out_2):
                 copy(out=stage[:, :, 2 * half : 2 * half + 2, :], in_=by_head)
             store(pair, unit, stage, 0, RUN)
 
-        def prepare_w(unit):
+        for unit in range(3):
             transpose_w(unit)
             group_w(unit)
-
-        prepare_w(0)
-        prepare_w(1)
         for chunk in range(TABLE_CHUNKS):
             add_table(0, chunk)
         quantise_w(0)
         for r in range(RUN):
             quantise_tokens(0, r)
         quantise_w(1)
-        project(0, 0, True)
-        prepare_w(2)
-        project(0, 1, True)
-        quantise_w(2)
-        add_table(1, 0)
-        prepare_w(3)
-        project(0, 2, False)
-        quantise_w(3)
-        add_table(1, 1)
-        prepare_w(4)
-        project(0, 3, True)
-        quantise_w(4)
-        add_table(1, 2)
-        project(0, 4, False)
-        add_table(1, 3)
+        for unit in range(UNITS):
+            project(0, unit, unit != 1)
+            if 1 <= unit and unit + 2 < UNITS:
+                group_w(unit + 2)
+            if unit + 3 < UNITS:
+                transpose_w(unit + 3)
+            if 1 <= unit and unit + 1 < UNITS:
+                quantise_w(unit + 1)
+                add_table(1, unit - 1)
         for r in range(RUN):
             quantise_tokens(1, r)
-        for unit in range(UNITS - 1):
+        for unit in range(UNITS):
             project(1, unit, True)
-            if unit == 0:
-                prepare_w(UNITS - 1)
-                quantise_w(UNITS - 1)
-        for pair in range(PAIRS):
-            project(pair, UNITS - 1, True)

@@ -65,7 +65,7 @@ def tile_multiheadselfattention_pa_kernel(tc, x, W_qkv, out_0, out_1, out_2):
             nc.sync.dma_start(
                 out=w_rows[:, unit],
                 in_=W_qkv[unit * UNIT_COLS : (unit + 1) * UNIT_COLS, :].rearrange(
-                    "(o g) c -> o g c", o=P
+                    "(g o) c -> o g c", o=P
                 ),
             )
 
@@ -187,8 +187,8 @@ def tile_multiheadselfattention_pa_kernel(tc, x, W_qkv, out_0, out_1, out_2):
 
         def group_w(unit):
             nc.scalar.copy(
-                out=w_grouped[:, unit].bitcast(F32).rearrange("q (o g) u -> q o g u", g=UNIT_BLOCKS),
-                in_=flipped_w[unit][:].rearrange("q g u o -> q o g u"),
+                out=w_grouped[:, unit].bitcast(F32).rearrange("q (g o) u -> q g o u", g=UNIT_BLOCKS),
+                in_=flipped_w[unit][:].rearrange("q g u o -> q g o u"),
             )
 
         def quantise_w(unit):
@@ -265,15 +265,16 @@ def tile_multiheadselfattention_pa_kernel(tc, x, W_qkv, out_0, out_1, out_2):
             quantise_tokens(0, r)
         quantise_w(1)
         for unit in range(UNITS):
-            project(0, unit, unit != 1)
-            if 1 <= unit and unit + 2 < UNITS:
-                group_w(unit + 2)
+            project(0, unit, unit not in (1, 3))
             if unit + 3 < UNITS:
                 transpose_w(unit + 3)
-            if 1 <= unit and unit + 1 < UNITS:
-                quantise_w(unit + 1)
-                add_table(1, unit - 1)
-        for r in range(RUN):
-            quantise_tokens(1, r)
+                group_w(unit + 3)
+            if unit + 2 < UNITS:
+                quantise_w(unit + 2)
+            if unit < TABLE_CHUNKS:
+                add_table(1, unit)
+            if unit == TABLE_CHUNKS:
+                for r in range(RUN):
+                    quantise_tokens(1, r)
         for unit in range(UNITS):
             project(1, unit, True)

@@ -89,30 +89,36 @@ def tile_multiheadselfattention_pa_kernel(tc, x, W_qkv, out_0, out_1, out_2):
 
         position = keep.tile([P, TABLE_CHUNKS, CHUNK], F32)
         iota(position[:], [[CHUNK, TABLE_CHUNKS], [1, CHUNK]], 0)
-        chan = keep.tile([P, 1], F32)
-        iota(chan[:], [[1, 1]], PACK)
-        base = keep.tile([P, 1], F32)
-        nc.vector.memset(base[:], 10000.0)
-        cosine = keep.tile([P, 1], F32)
-        nc.vector.memset(cosine[0:HALF_P], 0.0)
-        nc.vector.memset(cosine[HALF_P:P], 1.0)
-        exponent = keep.tile([P, 1], F32)
-        nc.gpsimd.tensor_scalar(
-            out=exponent[:],
-            in0=chan[:],
-            scalar1=-1.0 / RATES,
-            scalar2=cosine[:],
-            op0=ALU.mult,
-            op1=ALU.add,
-        )
-        rate = keep.tile([P, 1], F32)
-        nc.gpsimd.tensor_tensor(out=rate[:], in0=base[:], in1=exponent[:], op=ALU.pow)
         index = keep.tile([P, 1], F32)
         iota(index[:], [[1, 1]], 1)
 
         warm = keep.tile([P, 2], F32)
         nc.vector.memset(warm[:, 0:1], 0.0)
         nc.scalar.activation(out=warm[:, 1:2], in_=warm[:, 0:1], func=ACT.Sin)
+
+        ones = keep.tile([P, HALF_P], F32)
+        nc.vector.memset(ones[:], 1.0)
+        rate_row = keep.tile([P, P + HALF_P], F32)
+        nc.vector.memset(rate_row[:], 0.0)
+        ratio = keep.tile([1, HALF_P], F32)
+        nc.vector.tensor_scalar_mul(
+            out=ratio[:], in0=ones[0:1, :], scalar1=10000.0 ** (-PACK / RATES)
+        )
+        for first in (0, HALF_P):
+            nc.vector.tensor_tensor_scan(
+                out=rate_row[0:1, first : first + HALF_P],
+                data0=ratio[:],
+                data1=rate_row[0:1, P : P + HALF_P],
+                initial=10000.0 ** (PACK / RATES),
+                op0=ALU.mult,
+                op1=ALU.add,
+            )
+        rates = psum.tile([P, 2], F32, tag="bank")
+        nc.tensor.matmul(rates[:], lhsT=rate_row[:, 0:P], rhs=ones[:, 0:2], start=True, stop=True)
+
+        cosine = keep.tile([P, 1], F32)
+        nc.vector.memset(cosine[0:HALF_P], 0.0)
+        nc.vector.memset(cosine[HALF_P:P], 1.0)
         phase = keep.tile([P, 1], F32)
         nc.vector.tensor_scalar_mul(out=phase[:], in0=cosine[:], scalar1=0.25)
         phase_angle = keep.tile([P, 1], F32)
@@ -124,6 +130,9 @@ def tile_multiheadselfattention_pa_kernel(tc, x, W_qkv, out_0, out_1, out_2):
                 in0=position[:],
                 scalar1=10000.0 ** (-t / RATES) / (2.0 * math.pi),
             )
+
+        rate = keep.tile([P, 1], F32)
+        nc.vector.tensor_copy(out=rate[:], in_=rates[:, 0:1])
 
         whole = keep.tile([P, TABLE_CHUNKS, PACK, CHUNK], I32)
         frac = keep.tile([P, TABLE_CHUNKS, PACK, CHUNK], F32)

@@ -19,6 +19,8 @@ IMAGES = 4
 CHANNELS = 512
 POSITIONS = 256
 HEAD_DIM = 64
+BANK = 512
+WARM_UPS = 5
 
 PAIR = 2
 PAIRS = IMAGES // PAIR
@@ -92,33 +94,41 @@ def tile_multiheadselfattention_pa_kernel(tc, x, W_qkv, out_0, out_1, out_2):
         index = keep.tile([P, 1], F32)
         iota(index[:], [[1, 1]], 1)
 
-        warm = keep.tile([P, 2], F32)
-        nc.vector.memset(warm[:, 0:1], 0.0)
-        nc.scalar.activation(out=warm[:, 1:2], in_=warm[:, 0:1], func=ACT.Sin)
-
         ones = keep.tile([P, HALF_P], F32)
         nc.vector.memset(ones[:], 1.0)
-        rate_row = keep.tile([P, P + HALF_P], F32)
+        rate_row = keep.tile([P, P], F32)
         nc.vector.memset(rate_row[:], 0.0)
         ratio = keep.tile([1, HALF_P], F32)
         nc.vector.tensor_scalar_mul(
             out=ratio[:], in0=ones[0:1, :], scalar1=10000.0 ** (-PACK / RATES)
         )
+        warm = keep.tile([P, 2], F32)
+        nc.vector.memset(warm[:, 0:1], 0.0)
+        nc.scalar.activation(out=warm[:, 1:2], in_=warm[:, 0:1], func=ACT.Sin)
+        cosine = keep.tile([P, 1], F32)
+        nc.vector.memset(cosine[0:HALF_P], 0.0)
+        nc.vector.memset(cosine[HALF_P:P], 1.0)
         for first in (0, HALF_P):
             nc.vector.tensor_tensor_scan(
                 out=rate_row[0:1, first : first + HALF_P],
                 data0=ratio[:],
-                data1=rate_row[0:1, P : P + HALF_P],
+                data1=ones[0:1, :],
                 initial=10000.0 ** (PACK / RATES),
                 op0=ALU.mult,
-                op1=ALU.add,
+                op1=ALU.mult,
             )
         rates = psum.tile([P, 2], F32, tag="bank")
-        nc.tensor.matmul(rates[:], lhsT=rate_row[:, 0:P], rhs=ones[:, 0:2], start=True, stop=True)
+        nc.tensor.matmul(rates[:], lhsT=rate_row[:], rhs=ones[:, 0:2], start=True, stop=True)
+        zeros = keep.tile([P, BANK], BF16)
+        nc.gpsimd.memset(zeros[:], 0.0)
+        idle = psum.tile([P, BANK], F32, tag="bank")
 
-        cosine = keep.tile([P, 1], F32)
-        nc.vector.memset(cosine[0:HALF_P], 0.0)
-        nc.vector.memset(cosine[HALF_P:P], 1.0)
+        def warm_up(times):
+            for turn in range(times):
+                nc.tensor.matmul(idle[:], lhsT=zeros[:, 0:P], rhs=zeros[:], start=True, stop=True)
+
+        warm_up(WARM_UPS)
+
         phase = keep.tile([P, 1], F32)
         nc.vector.tensor_scalar_mul(out=phase[:], in0=cosine[:], scalar1=0.25)
         phase_angle = keep.tile([P, 1], F32)
@@ -266,6 +276,8 @@ def tile_multiheadselfattention_pa_kernel(tc, x, W_qkv, out_0, out_1, out_2):
 
         for unit in range(3):
             transpose_w(unit)
+            if unit == 1:
+                warm_up(1)
             group_w(unit)
         for chunk in range(TABLE_CHUNKS):
             add_table(0, chunk)

@@ -30,6 +30,7 @@ TABLE_CHUNKS = 4
 CHUNK = POSITIONS // TABLE_CHUNKS
 CHUNK_ROWS = ROWS // TABLE_CHUNKS
 
+HEADS = 8
 UNIT_HEADS = 4
 UNIT_COLS = UNIT_HEADS * HEAD_DIM
 UNIT_BLOCKS = UNIT_COLS // P
@@ -46,7 +47,7 @@ def tile_multiheadselfattention_pa_kernel(tc, x, W_qkv, out_0, out_1, out_2):
     outs = (out_0, out_1, out_2)
     with ExitStack() as pools:
         keep = pools.enter_context(tc.tile_pool(name="keep", bufs=1))
-        stage_pool = pools.enter_context(tc.tile_pool(name="stage", bufs=12))
+        stage_pool = pools.enter_context(tc.tile_pool(name="stage", bufs=6))
         psum = pools.enter_context(tc.psum_pool(name="psum", bufs=8))
         pools.enter_context(tc.manual_schedule())
 
@@ -255,28 +256,35 @@ def tile_multiheadselfattention_pa_kernel(tc, x, W_qkv, out_0, out_1, out_2):
                 )
             return acc[:].rearrange("m k (h d) -> m h k d", d=HEAD_DIM)
 
-        def store(pair, unit, stage, first, last):
-            first_head = (unit % UNITS_PER_OUTPUT) * UNIT_HEADS
+        def store(pair, output, stage, heads):
             for b in range(PAIR):
                 nc.sync.dma_start(
-                    out=outs[unit // UNITS_PER_OUTPUT][
-                        pair * PAIR + b, first_head : first_head + UNIT_HEADS
-                    ].rearrange("h (i r) d -> i h r d", r=RUN)[:, :, first:last, :]
-                    .rearrange("i h r d -> i h (r d)"),
-                    in_=stage[b:P:PAIR, :, first:last, :].rearrange("m h r d -> m h (r d)"),
+                    out=outs[output][pair * PAIR + b, heads].rearrange(
+                        "h (i r) d -> i h (r d)", r=RUN
+                    ),
+                    in_=stage[b:P:PAIR, heads].rearrange("m h r d -> m h (r d)"),
                 )
 
-        def project(pair, unit, vector_helps):
-            stage = stage_pool.tile([P, UNIT_HEADS, RUN, HEAD_DIM], F32)
+        stages = {}
+
+        def project(pair, unit, vector_helps, store_alone):
+            output, part = divmod(unit, UNITS_PER_OUTPUT)
+            if part == 0:
+                stages[pair, output] = stage_pool.tile([P, HEADS, RUN, HEAD_DIM], F32, name="stage")
+            stage = stages[pair, output]
+            heads = slice(part * UNIT_HEADS, (part + 1) * UNIT_HEADS)
             for half in range(2):
                 by_head = multiply(pair, unit, half)
                 copy = nc.vector.tensor_copy if vector_helps and half == 1 else nc.scalar.copy
-                copy(out=stage[:, :, 2 * half : 2 * half + 2, :], in_=by_head)
-            store(pair, unit, stage, 0, RUN)
+                copy(out=stage[:, heads, 2 * half : 2 * half + 2, :], in_=by_head)
+            if store_alone:
+                store(pair, output, stage, heads)
+            elif part == UNITS_PER_OUTPUT - 1:
+                store(pair, output, stage, slice(0, HEADS))
 
         for unit in range(3):
             transpose_w(unit)
-            if unit == 1:
+            if unit > 0:
                 warm_up(1)
             group_w(unit)
         for chunk in range(TABLE_CHUNKS):
@@ -286,7 +294,7 @@ def tile_multiheadselfattention_pa_kernel(tc, x, W_qkv, out_0, out_1, out_2):
             quantise_tokens(0, r)
         quantise_w(1)
         for unit in range(UNITS):
-            project(0, unit, unit not in (1, 3))
+            project(0, unit, unit not in (1, 3), True)
             if unit + 3 < UNITS:
                 transpose_w(unit + 3)
                 group_w(unit + 3)
@@ -298,4 +306,4 @@ def tile_multiheadselfattention_pa_kernel(tc, x, W_qkv, out_0, out_1, out_2):
                 for r in range(RUN):
                     quantise_tokens(1, r)
         for unit in range(UNITS):
-            project(1, unit, True)
+            project(1, unit, True, False)

import math
from contextlib import ExitStack

import concourse.mybir as mybir

F32 = mybir.dt.float32
BF16 = mybir.dt.bfloat16
I32 = mybir.dt.int32
U32 = mybir.dt.uint32
U8 = mybir.dt.uint8
FP8X4 = mybir.dt.float8_e4m3fn_x4
ALU = mybir.AluOpType
ACT = mybir.ActivationFunctionType

P = 128
HALF_P = P // 2
PACK = 4
IMAGES = 4
CHANNELS = 512
POSITIONS = 256
HEAD_DIM = 64
BANK = 512
WARM_UPS = 5

PAIR = 2
PAIRS = IMAGES // PAIR
RUN = 4
ROWS = POSITIONS // RUN
TABLE_CHUNKS = 4
CHUNK = POSITIONS // TABLE_CHUNKS
CHUNK_ROWS = ROWS // TABLE_CHUNKS

HEADS = 8
UNIT_HEADS = 4
UNIT_COLS = UNIT_HEADS * HEAD_DIM
UNIT_BLOCKS = UNIT_COLS // P
UNITS = 6
UNITS_PER_OUTPUT = 2

RATES = CHANNELS // 2

FLOPS = 2 * IMAGES * POSITIONS * CHANNELS * UNITS * UNIT_COLS


def tile_multiheadselfattention_pa_kernel(tc, x, W_qkv, out_0, out_1, out_2):
    nc = tc.nc
    outs = (out_0, out_1, out_2)
    with ExitStack() as pools:
        keep = pools.enter_context(tc.tile_pool(name="keep", bufs=1))
        stage_pool = pools.enter_context(tc.tile_pool(name="stage", bufs=6))
        psum = pools.enter_context(tc.psum_pool(name="psum", bufs=8))
        pools.enter_context(tc.manual_schedule())

        x_rows = keep.tile([P, IMAGES * PACK, POSITIONS], BF16)
        w_rows = keep.tile([P, UNITS, UNIT_BLOCKS, CHANNELS], BF16)

        def load_x(pair):
            nc.sync.dma_start(
                out=x_rows[:, pair * PAIR * PACK : (pair + 1) * PAIR * PACK, :].rearrange(
                    "q (b t) n -> q b (t n)", b=PAIR
                ),
                in_=x[pair * PAIR : (pair + 1) * PAIR].rearrange(
                    "b (q t) h w -> q b (t h w)", t=PACK
                ),
            )

        def load_w(unit):
            nc.sync.dma_start(
                out=w_rows[:, unit],
                in_=W_qkv[unit * UNIT_COLS : (unit + 1) * UNIT_COLS, :].rearrange(
                    "(g o) c -> o g c", o=P
                ),
            )

        load_x(0)
        load_w(0)
        load_w(1)
        load_w(2)
        load_w(3)
        load_x(1)
        load_w(4)
        load_w(5)

        def iota(tile, pattern, channel_multiplier):
            nc.gpsimd.iota(
                tile,
                pattern=pattern,
                base=0,
                channel_multiplier=channel_multiplier,
                allow_small_or_imprecise_dtypes=True,
            )

        position = keep.tile([P, TABLE_CHUNKS, CHUNK], F32)
        iota(position[:], [[CHUNK, TABLE_CHUNKS], [1, CHUNK]], 0)
        index = keep.tile([P, 1], F32)
        iota(index[:], [[1, 1]], 1)

        ones = keep.tile([P, HALF_P], F32)
        nc.vector.memset(ones[:], 1.0)
        rate_row = keep.tile([P, P], F32)
        nc.vector.memset(rate_row[:], 0.0)
        ratio = keep.tile([1, HALF_P], F32)
        nc.vector.tensor_scalar_mul(
            out=ratio[:], in0=ones[0:1, :], scalar1=10000.0 ** (-PACK / RATES)
        )
        warm = keep.tile([P, 2], F32)
        nc.vector.memset(warm[:, 0:1], 0.0)
        nc.scalar.activation(out=warm[:, 1:2], in_=warm[:, 0:1], func=ACT.Sin)
        cosine = keep.tile([P, 1], F32)
        nc.vector.memset(cosine[0:HALF_P], 0.0)
        nc.vector.memset(cosine[HALF_P:P], 1.0)
        for first in (0, HALF_P):
            nc.vector.tensor_tensor_scan(
                out=rate_row[0:1, first : first + HALF_P],
                data0=ratio[:],
                data1=ones[0:1, :],
                initial=10000.0 ** (PACK / RATES),
                op0=ALU.mult,
                op1=ALU.mult,
            )
        rates = psum.tile([P, 2], F32, tag="bank")
        nc.tensor.matmul(rates[:], lhsT=rate_row[:], rhs=ones[:, 0:2], start=True, stop=True)
        zeros = keep.tile([P, BANK], BF16)
        nc.gpsimd.memset(zeros[:], 0.0)
        idle = psum.tile([P, BANK], F32, tag="bank")

        def warm_up(times):
            for turn in range(times):
                nc.tensor.matmul(idle[:], lhsT=zeros[:, 0:P], rhs=zeros[:], start=True, stop=True)

        warm_up(WARM_UPS)

        phase = keep.tile([P, 1], F32)
        nc.vector.tensor_scalar_mul(out=phase[:], in0=cosine[:], scalar1=0.25)
        phase_angle = keep.tile([P, 1], F32)
        nc.vector.tensor_scalar_mul(out=phase_angle[:], in0=cosine[:], scalar1=0.5 * math.pi)
        steps = keep.tile([P, TABLE_CHUNKS, PACK, CHUNK], F32)
        for t in range(PACK):
            nc.vector.tensor_scalar_mul(
                out=steps[:, :, t, :],
                in0=position[:],
                scalar1=10000.0 ** (-t / RATES) / (2.0 * math.pi),
            )

        rate = keep.tile([P, 1], F32)
        nc.vector.tensor_copy(out=rate[:], in_=rates[:, 0:1])

        whole = keep.tile([P, TABLE_CHUNKS, PACK, CHUNK], I32)
        frac = keep.tile([P, TABLE_CHUNKS, PACK, CHUNK], F32)
        pe = keep.tile([P, PAIR * PACK, POSITIONS], F32)

        def whole_turns(chunk):
            nc.vector.tensor_scalar(
                out=whole[:, chunk].rearrange("q t n -> q (t n)"),
                in0=steps[:, chunk].rearrange("q t n -> q (t n)"),
                scalar1=rate[:],
                scalar2=phase[:],
                op0=ALU.mult,
                op1=ALU.add,
            )

        def take_away(chunk):
            nc.vector.scalar_tensor_tensor(
                out=frac[:, chunk].rearrange("q t n -> q (t n)"),
                in0=steps[:, chunk].rearrange("q t n -> q (t n)"),
                scalar=rate[:],
                in1=whole[:, chunk].rearrange("q t n -> q (t n)"),
                op0=ALU.mult,
                op1=ALU.subtract,
            )
            nc.scalar.activation(
                out=pe[:, :, chunk * CHUNK : (chunk + 1) * CHUNK].rearrange(
                    "q (b t) n -> q b t n", b=PAIR
                ),
                in_=frac[:, chunk].unsqueeze(1).to_broadcast([P, PAIR, PACK, CHUNK]),
                func=ACT.Sin,
                scale=2.0 * math.pi,
                bias=phase_angle[:],
            )

        whole_turns(0)
        for chunk in range(TABLE_CHUNKS):
            if chunk + 1 < TABLE_CHUNKS:
                whole_turns(chunk + 1)
            take_away(chunk)
        ident = keep.tile([P, P], F32)
        nc.vector.tensor_scalar(
            out=ident[:],
            in0=position[:].rearrange("q c n -> q (c n)")[:, 0:P],
            scalar1=index[:],
            scalar2=None,
            op0=ALU.is_equal,
        )

        w_grouped = keep.tile([P, UNITS, UNIT_COLS, PACK], BF16, align_bytes=64)
        w_codes = keep.tile([P, UNITS, UNIT_COLS], U32, align_bytes=64)
        w_scales = keep.tile([P, UNITS, UNIT_COLS], U8, align_bytes=64)
        flipped_w = {}

        def transpose_w(unit):
            words = w_rows[:, unit].bitcast(F32)
            flipped = psum.tile([P, UNIT_BLOCKS, 2, P], F32, tag="bank")
            for g in range(UNIT_BLOCKS):
                for u in range(2):
                    nc.tensor.transpose(flipped[:, g, u, :], words[:, g, u : 2 * P : 2], ident[:])
            flipped_w[unit] = flipped

        def group_w(unit):
            nc.scalar.copy(
                out=w_grouped[:, unit].bitcast(F32).rearrange("q (g o) u -> q g o u", g=UNIT_BLOCKS),
                in_=flipped_w[unit][:].rearrange("q g u o -> q g o u"),
            )

        def quantise_w(unit):
            nc.vector.quantize_mx(
                out=w_codes[:, unit, :].bitcast(FP8X4),
                scales=w_scales[:, unit, :],
                in_=w_grouped[:, unit].rearrange("q c t -> q (c t)"),
            )

        tok = keep.tile([P, PAIRS, RUN, ROWS, PAIR * PACK], BF16, align_bytes=64)
        tok_codes = keep.tile([P, PAIRS, RUN * P], U32, align_bytes=64)
        tok_scales = keep.tile([P, PAIRS, RUN * P], U8, align_bytes=64)

        def add_table(pair, chunk):
            span = slice(chunk * CHUNK, (chunk + 1) * CHUNK)
            rows = slice(chunk * CHUNK_ROWS, (chunk + 1) * CHUNK_ROWS)
            nc.vector.tensor_tensor(
                out=tok[:, pair, :, rows, :].rearrange("q r i g -> q i g r"),
                in0=x_rows[:, pair * PAIR * PACK : (pair + 1) * PAIR * PACK, span].rearrange(
                    "q g (i r) -> q i g r", r=RUN
                ),
                in1=pe[:, :, span].rearrange("q g (i r) -> q i g r", r=RUN),
                op=ALU.add,
            )

        def quantise_tokens(pair, r):
            nc.vector.quantize_mx(
                out=tok_codes[:, pair, r * P : (r + 1) * P].bitcast(FP8X4),
                scales=tok_scales[:, pair, r * P : (r + 1) * P],
                in_=tok[:, pair, r].rearrange("q i g -> q (i g)"),
            )

        def multiply(pair, unit, half):
            acc = psum.tile([P, 2, UNIT_COLS], F32, tag="bank")
            for k in range(2):
                r = 2 * half + k
                nc.tensor.matmul_mx(
                    out=acc[:, k, :],
                    lhsT=tok_codes[:, pair, r * P : (r + 1) * P].bitcast(FP8X4),
                    lhsT_scale=tok_scales[:, pair, r * P : (r + 1) * P],
                    rhs=w_codes[:, unit, :].bitcast(FP8X4),
                    rhs_scale=w_scales[:, unit, :],
                    start=True,
                    stop=True,
                )
            return acc[:].rearrange("m k (h d) -> m h k d", d=HEAD_DIM)

        def store(pair, output, stage, heads):
            for b in range(PAIR):
                nc.sync.dma_start(
                    out=outs[output][pair * PAIR + b, heads].rearrange(
                        "h (i r) d -> i h (r d)", r=RUN
                    ),
                    in_=stage[b:P:PAIR, heads].rearrange("m h r d -> m h (r d)"),
                )

        stages = {}

        def project(pair, unit, vector_helps, store_alone):
            output, part = divmod(unit, UNITS_PER_OUTPUT)
            if part == 0:
                stages[pair, output] = stage_pool.tile([P, HEADS, RUN, HEAD_DIM], F32, name="stage")
            stage = stages[pair, output]
            heads = slice(part * UNIT_HEADS, (part + 1) * UNIT_HEADS)
            for half in range(2):
                by_head = multiply(pair, unit, half)
                copy = nc.vector.tensor_copy if vector_helps and half == 1 else nc.scalar.copy
                copy(out=stage[:, heads, 2 * half : 2 * half + 2, :], in_=by_head)
            if store_alone:
                store(pair, output, stage, heads)
            elif part == UNITS_PER_OUTPUT - 1:
                store(pair, output, stage, slice(0, HEADS))

        for unit in range(3):
            transpose_w(unit)
            if unit > 0:
                warm_up(1)
            group_w(unit)
        for chunk in range(TABLE_CHUNKS):
            add_table(0, chunk)
        quantise_w(0)
        for r in range(RUN):
            quantise_tokens(0, r)
        quantise_w(1)
        for unit in range(UNITS):
            project(0, unit, unit not in (1, 3), True)
            if unit + 3 < UNITS:
                transpose_w(unit + 3)
                group_w(unit + 3)
            if unit + 2 < UNITS:
                quantise_w(unit + 2)
            if unit < TABLE_CHUNKS:
                add_table(1, unit)
            if unit == TABLE_CHUNKS:
                for r in range(RUN):
                    quantise_tokens(1, r)
        for unit in range(UNITS):
            project(1, unit, True, False)
